import numpy as np
import ml_dtypes


def mxq(x, axis, fmt="e4m3"):
    dtype, down = {"e4m3": (ml_dtypes.float8_e4m3fn, 7), "e5m2": (ml_dtypes.float8_e5m2, 14)}[fmt]
    v = np.moveaxis(np.asarray(x, np.float32).astype(ml_dtypes.bfloat16).astype(np.float64), axis, -1)
    blocks = v.reshape(v.shape[:-1] + (-1, 32))
    amax = np.abs(blocks).max(-1, keepdims=True)
    byte = np.maximum(np.where(amax > 0, np.frexp(amax)[1] - 1 + 127, 0) - down, 1)
    scale = np.exp2(byte - 127.0)
    codes = (blocks / scale).astype(np.float32).astype(dtype).astype(np.float64)
    return np.moveaxis((codes * scale).reshape(v.shape), -1, axis)


WIDE = False


def mx_kscale(k):
    if not WIDE:
        return np.ones(k)
    levels = np.array([20, -20, 10, -10, 0])
    a = np.random.permutation(np.resize(levels, k // 512 * 4)).reshape(k // 512, 4)
    idx = np.arange(k)
    return np.exp2(a[idx // 512, idx % 128 // 32])


BF16 = ml_dtypes.bfloat16


def bf(x):
    return np.asarray(x, np.float32).astype(BF16)


def f64(x):
    return np.asarray(x).astype(np.float64)


B, V, K, C = 8, 2048, 512, 512


def setup_inputs():
    s = mx_kscale(V)
    u = np.sqrt(s)[:, None]
    evals = np.random.uniform(0.0, 4.0, (B, K))
    evecs = np.random.standard_normal((B, V, K)) * 2.0 / np.sqrt(K) * u
    g = np.random.standard_normal((B, V, C)) * np.exp2(np.random.randint(-12, 1, (B, V, 1))) * 8.0 / (u * u)
    return {"evals": bf(evals), "evecs": bf(evecs), "count": C, "grad_out": bf(g)}


def reference(evals, evecs, count, grad_out):
    scales = 10.0 ** np.linspace(-2.0, 0.0, count)
    coefs = np.exp(-f64(evals)[:, None, :] * scales[None, :, None])
    ev = f64(evecs)
    sq = ev * ev
    d = mxq(f64(grad_out), 1, "e5m2").transpose(0, 2, 1) @ mxq(sq, 1, "e4m3")
    return -np.sum(d * coefs * scales[None, :, None], axis=1)

@@ -1,0 +1,194 @@
+import math
+from contextlib import ExitStack
+
+import concourse.mybir as mybir
+from concourse.masks import make_identity
+
+F32 = mybir.dt.float32
+BF16 = mybir.dt.bfloat16
+U32 = mybir.dt.uint32
+U8 = mybir.dt.uint8
+I32 = mybir.dt.int32
+E4 = mybir.dt.float8_e4m3fn_x4
+E5 = mybir.dt.float8_e5m2_x4
+ACT = mybir.ActivationFunctionType
+ALU = mybir.AluOpType
+
+P = 128
+PACK = 4
+K_PASS = P * PACK
+
+FLOPS = 2 * 8 * 512 * 512 * 2048
+
+RAW_BUFS = 8
+BANKS = 7
+
+
+def tile_hks_kernel(tc, evals, evecs, count, grad_out, out):
+    nc = tc.nc
+    n_b, n_v, n_k = evecs.shape
+    n_c = grad_out.shape[2]
+    assert count == n_c and n_k == 512 and n_c == 512 and n_v % K_PASS == 0
+    passes = n_v // K_PASS
+    c_tiles = n_c // P
+    width = PACK * n_k
+    chunks = n_b * passes
+
+    with ExitStack() as ctx:
+        const = ctx.enter_context(tc.tile_pool(name="const", bufs=1))
+        rawp = ctx.enter_context(tc.tile_pool(name="rawp", bufs=RAW_BUFS))
+        grpp = ctx.enter_context(tc.tile_pool(name="grpp", bufs=3))
+        codp = ctx.enter_context(tc.tile_pool(name="codp", bufs=4))
+        wgtp = ctx.enter_context(tc.tile_pool(name="wgtp", bufs=2 * c_tiles))
+        prdp = ctx.enter_context(tc.tile_pool(name="prdp", bufs=4))
+        bankp = ctx.enter_context(tc.psum_pool(name="bankp", bufs=1))
+        accp = ctx.enter_context(tc.psum_pool(name="accp", bufs=1))
+        ctx.enter_context(tc.manual_schedule())
+
+        g_raw, e_raw, g_grp, e_grp = {}, {}, {}, {}
+        g_cod, g_scl, e_cod, e_scl = {}, {}, {}, {}
+        lam_ps, wgt, d_ps = {}, {}, {}
+
+        def bank(index):
+            return bankp.tile([P, n_k], F32, name="bank%d" % (index % BANKS), tag="bank%d" % (index % BANKS))
+
+        def load(i):
+            b, vc = divmod(i, passes)
+            rows = slice(vc * K_PASS, (vc + 1) * K_PASS)
+            g_raw[i] = rawp.tile([P, width], BF16, name="g_raw", tag="g_raw")
+            nc.sync.dma_start(out=g_raw[i][:], in_=grad_out[b, rows, :].rearrange("(p j) w -> p (j w)", j=PACK))
+            e_raw[i] = rawp.tile([P, width], BF16, name="e_raw", tag="e_raw")
+            nc.sync.dma_start(out=e_raw[i][:], in_=evecs[b, rows, :].rearrange("(p j) w -> p (j w)", j=PACK))
+
+        def square(i):
+            e_grp[i] = grpp.tile([P, width], BF16, name="e_grp", tag="e_grp", align_bytes=64)
+            nc.scalar.activation(
+                out=e_grp[i][:].rearrange("p (c i t) -> p c t i", i=4, t=PACK),
+                in_=e_raw[i][:].rearrange("p (t c i) -> p c t i", t=PACK, i=4),
+                func=ACT.Square,
+            )
+
+        def regroup(i):
+            g_grp[i] = grpp.tile([P, width], BF16, name="g_grp", tag="g_grp", align_bytes=64)
+            nc.vector.tensor_copy(
+                out=g_grp[i][:].rearrange("p (c i t) -> p c t i", i=4, t=PACK),
+                in_=g_raw[i][:].rearrange("p (t c i) -> p c t i", t=PACK, i=4),
+            )
+
+        def quantise_g(i):
+            g_cod[i] = codp.tile([P, n_c], U32, name="g_cod", tag="g_cod", align_bytes=64)
+            g_scl[i] = codp.tile([P, n_c], U8, name="g_scl", tag="g_scl", align_bytes=64)
+            nc.vector.quantize_mx(out=g_cod[i][:].bitcast(E5), scales=g_scl[i][:], in_=g_grp[i][:])
+
+        def quantise_e(i):
+            e_cod[i] = codp.tile([P, n_k], U32, name="e_cod", tag="e_cod", align_bytes=64)
+            e_scl[i] = codp.tile([P, n_k], U8, name="e_scl", tag="e_scl", align_bytes=64)
+            nc.vector.quantize_mx(out=e_cod[i][:].bitcast(E4), scales=e_scl[i][:], in_=e_grp[i][:])
+
+        def mx_pass(i, ct):
+            b, vc = divmod(i, passes)
+            if vc == 0:
+                d_ps[b, ct] = bank(5 * b + 1 + ct)
+            cols = slice(ct * P, (ct + 1) * P)
+            nc.tensor.matmul_mx(
+                out=d_ps[b, ct][:],
+                lhsT=g_cod[i][:, cols].bitcast(E5), lhsT_scale=g_scl[i][:, cols],
+                rhs=e_cod[i][:].bitcast(E4), rhs_scale=e_scl[i][:],
+                start=(vc == 0), stop=(vc == passes - 1),
+            )
+
+        def spread_evals(b):
+            lam_ps[b] = bank(5 * b)
+            nc.tensor.matmul(
+                out=lam_ps[b][:], lhsT=ident[:, b : b + 1].to_broadcast([P, P]), rhs=lam8[:],
+                start=True, stop=True,
+            )
+
+        def weights(b):
+            for ct in range(c_tiles):
+                wgt[b, ct] = wgtp.tile([P, n_k], F32, name="wgt", tag="wgt")
+                nc.scalar.activation(
+                    out=wgt[b, ct][:], in_=lam_ps[b][:], func=ACT.Exp,
+                    bias=lns[:, ct : ct + 1], scale=sneg[:, ct : ct + 1],
+                )
+
+        def weigh(b, ct):
+            prod = prdp.tile([P, n_k], F32, name="prod", tag="prod")
+            nc.vector.tensor_tensor(out=prod[:], in0=d_ps[b, ct][:], in1=wgt[b, ct][:], op=ALU.mult)
+            return prod
+
+        def reduce_c(b, prod, first, last):
+            nc.tensor.matmul(
+                out=acc[:], lhsT=selw[:, P - 1 - b : 2 * P - 1 - b], rhs=prod[:], start=first, stop=last,
+            )
+
+        lam8 = const.tile([P, n_k], BF16)
+        nc.vector.memset(lam8[:], 0.0)
+        nc.scalar.dma_start(out=lam8[0:n_b, :], in_=evals)
+        for i in range(RAW_BUFS):
+            load(i)
+        cidx = const.tile([P, c_tiles], I32)
+        nc.gpsimd.iota(cidx[:], pattern=[[P, c_tiles]], base=0, channel_multiplier=1)
+        ident = const.tile([P, P], BF16)
+        make_identity(nc, ident[:])
+        cflt = const.tile([P, c_tiles], F32)
+        nc.vector.tensor_copy(out=cflt[:], in_=cidx[:])
+        lns = const.tile([P, c_tiles], F32)
+        nc.vector.tensor_scalar(
+            out=lns[:], in0=cflt[:],
+            scalar1=2.0 * math.log(10.0) / (n_c - 1), scalar2=-2.0 * math.log(10.0),
+            op0=ALU.mult, op1=ALU.add,
+        )
+        spos = const.tile([P, c_tiles], F32)
+        nc.scalar.activation(out=spos[:], in_=lns[:], func=ACT.Exp)
+        sneg = const.tile([P, c_tiles], F32)
+        nc.vector.tensor_scalar_mul(out=sneg[:], in0=spos[:], scalar1=-1.0)
+        selw = const.tile([P, 2 * P], F32)
+        nc.vector.memset(selw[:], 0.0)
+        nc.vector.memset(selw[:, P - 1 : P], -1.0)
+        acc = accp.tile([P, n_k], F32)
+
+        spread_evals(0)
+        weights(0)
+        regroup(0)
+        square(0)
+        load(RAW_BUFS)
+
+        for i in range(chunks):
+            b, vc = divmod(i, passes)
+            if i + 1 < chunks:
+                regroup(i + 1)
+                square(i + 1)
+            if i + 1 + RAW_BUFS < chunks:
+                load(i + 1 + RAW_BUFS)
+            quantise_g(i)
+            quantise_e(i)
+            if vc == 0 and b > 0:
+                mx_pass(i, 0)
+                mx_pass(i, 1)
+                prods = [weigh(b - 1, 0)]
+                mx_pass(i, 2)
+                prods.append(weigh(b - 1, 1))
+                mx_pass(i, 3)
+                prods.append(weigh(b - 1, 2))
+                prods.append(weigh(b - 1, 3))
+                for ct in range(c_tiles):
+                    reduce_c(b - 1, prods[ct], b == 1 and ct == 0, False)
+                weights(b)
+            else:
+                for ct in range(c_tiles):
+                    mx_pass(i, ct)
+            if vc == passes - 1 and b + 1 < n_b:
+                spread_evals(b + 1)
+
+        b = n_b - 1
+        for ct in range(2):
+            reduce_c(b, weigh(b, ct), False, False)
+        prod2 = weigh(b, 2)
+        prod3 = weigh(b, 3)
+        nc.vector.tensor_tensor(out=prod3[:], in0=prod2[:], in1=prod3[:], op=ALU.add)
+        reduce_c(b, prod3, False, True)
+
+        res = const.tile([P, n_k], F32)
+        nc.scalar.copy(out=res[:], in_=acc[:])
+        nc.sync.dma_start(out=out, in_=res[0:n_b, :])

@@ -22,6 +22,7 @@ FLOPS = 2 * 8 * 512 * 512 * 2048
 
 RAW_BUFS = 8
 BANKS = 7
+GP_COLS = 0
 
 
 def tile_hks_kernel(tc, evals, evecs, count, grad_out, out):
@@ -37,7 +38,8 @@ def tile_hks_kernel(tc, evals, evecs, count, grad_out, out):
     with ExitStack() as ctx:
         const = ctx.enter_context(tc.tile_pool(name="const", bufs=1))
         rawp = ctx.enter_context(tc.tile_pool(name="rawp", bufs=RAW_BUFS))
-        grpp = ctx.enter_context(tc.tile_pool(name="grpp", bufs=3))
+        ggrp = ctx.enter_context(tc.tile_pool(name="ggrp", bufs=2))
+        egrp = ctx.enter_context(tc.tile_pool(name="egrp", bufs=3))
         codp = ctx.enter_context(tc.tile_pool(name="codp", bufs=4))
         wgtp = ctx.enter_context(tc.tile_pool(name="wgtp", bufs=2 * c_tiles))
         prdp = ctx.enter_context(tc.tile_pool(name="prdp", bufs=4))
@@ -47,7 +49,7 @@ def tile_hks_kernel(tc, evals, evecs, count, grad_out, out):
 
         g_raw, e_raw, g_grp, e_grp = {}, {}, {}, {}
         g_cod, g_scl, e_cod, e_scl = {}, {}, {}, {}
-        lam_ps, wgt, d_ps = {}, {}, {}
+        lam_ps, wgt, d_ps, prod = {}, {}, {}, {}
 
         def bank(index):
             return bankp.tile([P, n_k], F32, name="bank%d" % (index % BANKS), tag="bank%d" % (index % BANKS))
@@ -60,25 +62,38 @@ def tile_hks_kernel(tc, evals, evecs, count, grad_out, out):
             e_raw[i] = rawp.tile([P, width], BF16, name="e_raw", tag="e_raw")
             nc.sync.dma_start(out=e_raw[i][:], in_=evecs[b, rows, :].rearrange("(p j) w -> p (j w)", j=PACK))
 
+        def grouped(tile_ap, lo, hi):
+            return tile_ap[:, PACK * lo : PACK * hi].rearrange("p (c i t) -> p c t i", i=4, t=PACK)
+
+        def rowwise(tile_ap, lo, hi):
+            return tile_ap[:].rearrange("p (t w) -> p t w", t=PACK)[:, :, lo:hi].rearrange("p t (c i) -> p c t i", i=4)
+
         def square(i):
-            e_grp[i] = grpp.tile([P, width], BF16, name="e_grp", tag="e_grp", align_bytes=64)
-            nc.scalar.activation(
-                out=e_grp[i][:].rearrange("p (c i t) -> p c t i", i=4, t=PACK),
-                in_=e_raw[i][:].rearrange("p (t c i) -> p c t i", t=PACK, i=4),
-                func=ACT.Square,
+            e_grp[i] = egrp.tile([P, width], BF16, name="e_grp", tag="e_grp", align_bytes=64)
+            nc.scalar.activation(out=grouped(e_grp[i], 0, n_k), in_=rowwise(e_raw[i], 0, n_k), func=ACT.Square)
+
+        def regroup_gpsimd(i):
+            g_grp[i] = ggrp.tile([P, width], BF16, name="g_grp", tag="g_grp", align_bytes=64)
+            nc.gpsimd.tensor_scalar(
+                out=grouped(g_grp[i], 0, GP_COLS), in0=rowwise(g_raw[i], 0, GP_COLS),
+                scalar1=1.0, scalar2=0.0, op0=ALU.mult, op1=ALU.add,
             )
 
         def regroup(i):
-            g_grp[i] = grpp.tile([P, width], BF16, name="g_grp", tag="g_grp", align_bytes=64)
-            nc.vector.tensor_copy(
-                out=g_grp[i][:].rearrange("p (c i t) -> p c t i", i=4, t=PACK),
-                in_=g_raw[i][:].rearrange("p (t c i) -> p c t i", t=PACK, i=4),
-            )
+            lo = GP_COLS if i in g_grp else 0
+            if lo == 0:
+                g_grp[i] = ggrp.tile([P, width], BF16, name="g_grp", tag="g_grp", align_bytes=64)
+            nc.vector.tensor_copy(out=grouped(g_grp[i], lo, n_c), in_=rowwise(g_raw[i], lo, n_c))
 
-        def quantise_g(i):
+        def quantise_g(i, pieces):
             g_cod[i] = codp.tile([P, n_c], U32, name="g_cod", tag="g_cod", align_bytes=64)
             g_scl[i] = codp.tile([P, n_c], U8, name="g_scl", tag="g_scl", align_bytes=64)
-            nc.vector.quantize_mx(out=g_cod[i][:].bitcast(E5), scales=g_scl[i][:], in_=g_grp[i][:])
+            step = n_c // pieces
+            for lo in range(0, n_c, step):
+                nc.vector.quantize_mx(
+                    out=g_cod[i][:, lo : lo + step].bitcast(E5), scales=g_scl[i][:, lo : lo + step],
+                    in_=g_grp[i][:, PACK * lo : PACK * (lo + step)],
+                )
 
         def quantise_e(i):
             e_cod[i] = codp.tile([P, n_k], U32, name="e_cod", tag="e_cod", align_bytes=64)
@@ -113,18 +128,18 @@ def tile_hks_kernel(tc, evals, evecs, count, grad_out, out):
                 )
 
         def weigh(b, ct):
-            prod = prdp.tile([P, n_k], F32, name="prod", tag="prod")
-            nc.vector.tensor_tensor(out=prod[:], in0=d_ps[b, ct][:], in1=wgt[b, ct][:], op=ALU.mult)
-            return prod
+            prod[b, ct] = prdp.tile([P, n_k], F32, name="prod", tag="prod")
+            nc.vector.tensor_tensor(out=prod[b, ct][:], in0=d_ps[b, ct][:], in1=wgt[b, ct][:], op=ALU.mult)
 
-        def reduce_c(b, prod, first, last):
+        def reduce_c(b, ct):
             nc.tensor.matmul(
-                out=acc[:], lhsT=selw[:, P - 1 - b : 2 * P - 1 - b], rhs=prod[:], start=first, stop=last,
+                out=acc[:], lhsT=selw[:, P - 1 - b : 2 * P - 1 - b], rhs=prod[b, ct][:],
+                start=(b == 0 and ct == 0), stop=(b == n_b - 1 and ct == c_tiles - 1),
             )
 
         lam8 = const.tile([P, n_k], BF16)
         nc.vector.memset(lam8[:], 0.0)
-        nc.scalar.dma_start(out=lam8[0:n_b, :], in_=evals)
+        nc.sync.dma_start(out=lam8[0:n_b, :], in_=evals)
         for i in range(RAW_BUFS):
             load(i)
         cidx = const.tile([P, c_tiles], I32)
@@ -141,11 +156,11 @@ def tile_hks_kernel(tc, evals, evecs, count, grad_out, out):
         )
         spos = const.tile([P, c_tiles], F32)
         nc.scalar.activation(out=spos[:], in_=lns[:], func=ACT.Exp)
-        sneg = const.tile([P, c_tiles], F32)
-        nc.vector.tensor_scalar_mul(out=sneg[:], in0=spos[:], scalar1=-1.0)
         selw = const.tile([P, 2 * P], F32)
         nc.vector.memset(selw[:], 0.0)
         nc.vector.memset(selw[:, P - 1 : P], -1.0)
+        sneg = const.tile([P, c_tiles], F32)
+        nc.vector.tensor_scalar_mul(out=sneg[:], in0=spos[:], scalar1=-1.0)
         acc = accp.tile([P, n_k], F32)
 
         spread_evals(0)
@@ -153,6 +168,7 @@ def tile_hks_kernel(tc, evals, evecs, count, grad_out, out):
         regroup(0)
         square(0)
         load(RAW_BUFS)
+        quantise_g(0, 1)
 
         for i in range(chunks):
             b, vc = divmod(i, passes)
@@ -161,19 +177,24 @@ def tile_hks_kernel(tc, evals, evecs, count, grad_out, out):
                 square(i + 1)
             if i + 1 + RAW_BUFS < chunks:
                 load(i + 1 + RAW_BUFS)
-            quantise_g(i)
             quantise_e(i)
+            if i + 1 < chunks - 1:
+                quantise_g(i + 1, 1)
+            if i == chunks - 1:
+                quantise_g(i, c_tiles)
             if vc == 0 and b > 0:
+                if GP_COLS > 0 and i + 3 < chunks:
+                    regroup_gpsimd(i + 3)
                 mx_pass(i, 0)
                 mx_pass(i, 1)
-                prods = [weigh(b - 1, 0)]
+                weigh(b - 1, 0)
                 mx_pass(i, 2)
-                prods.append(weigh(b - 1, 1))
+                weigh(b - 1, 1)
                 mx_pass(i, 3)
-                prods.append(weigh(b - 1, 2))
-                prods.append(weigh(b - 1, 3))
+                weigh(b - 1, 2)
+                weigh(b - 1, 3)
                 for ct in range(c_tiles):
-                    reduce_c(b - 1, prods[ct], b == 1 and ct == 0, False)
+                    reduce_c(b - 1, ct)
                 weights(b)
             else:
                 for ct in range(c_tiles):
@@ -183,11 +204,12 @@ def tile_hks_kernel(tc, evals, evecs, count, grad_out, out):
 
         b = n_b - 1
         for ct in range(2):
-            reduce_c(b, weigh(b, ct), False, False)
-        prod2 = weigh(b, 2)
-        prod3 = weigh(b, 3)
-        nc.vector.tensor_tensor(out=prod3[:], in0=prod2[:], in1=prod3[:], op=ALU.add)
-        reduce_c(b, prod3, False, True)
+            weigh(b, ct)
+            reduce_c(b, ct)
+        weigh(b, 2)
+        weigh(b, 3)
+        nc.vector.tensor_tensor(out=prod[b, 3][:], in0=prod[b, 2][:], in1=prod[b, 3][:], op=ALU.add)
+        reduce_c(b, 3)
 
         res = const.tile([P, n_k], F32)
         nc.scalar.copy(out=res[:], in_=acc[:])

@@ -22,7 +22,7 @@ FLOPS = 2 * 8 * 512 * 512 * 2048
 
 RAW_BUFS = 8
 BANKS = 7
-GP_COLS = 0
+GP_COLS = 320
 
 
 def tile_hks_kernel(tc, evals, evecs, count, grad_out, out):

@@ -23,6 +23,7 @@ FLOPS = 2 * 8 * 512 * 512 * 2048
 RAW_BUFS = 8
 BANKS = 7
 GP_COLS = 320
+V_SQUARES = {}
 
 
 def tile_hks_kernel(tc, evals, evecs, count, grad_out, out):
@@ -54,13 +55,21 @@ def tile_hks_kernel(tc, evals, evecs, count, grad_out, out):
         def bank(index):
             return bankp.tile([P, n_k], F32, name="bank%d" % (index % BANKS), tag="bank%d" % (index % BANKS))
 
-        def load(i):
+        def load_g(i):
             b, vc = divmod(i, passes)
             rows = slice(vc * K_PASS, (vc + 1) * K_PASS)
             g_raw[i] = rawp.tile([P, width], BF16, name="g_raw", tag="g_raw")
             nc.sync.dma_start(out=g_raw[i][:], in_=grad_out[b, rows, :].rearrange("(p j) w -> p (j w)", j=PACK))
+
+        def load_e(i):
+            b, vc = divmod(i, passes)
+            rows = slice(vc * K_PASS, (vc + 1) * K_PASS)
             e_raw[i] = rawp.tile([P, width], BF16, name="e_raw", tag="e_raw")
             nc.sync.dma_start(out=e_raw[i][:], in_=evecs[b, rows, :].rearrange("(p j) w -> p (j w)", j=PACK))
+
+        def load(i):
+            load_g(i)
+            load_e(i)
 
         def grouped(tile_ap, lo, hi):
             return tile_ap[:, PACK * lo : PACK * hi].rearrange("p (c i t) -> p c t i", i=4, t=PACK)
@@ -69,13 +78,23 @@ def tile_hks_kernel(tc, evals, evecs, count, grad_out, out):
             return tile_ap[:].rearrange("p (t w) -> p t w", t=PACK)[:, :, lo:hi].rearrange("p t (c i) -> p c t i", i=4)
 
         def square(i):
+            hi = n_k - V_SQUARES.get(i, 0)
             e_grp[i] = egrp.tile([P, width], BF16, name="e_grp", tag="e_grp", align_bytes=64)
-            nc.scalar.activation(out=grouped(e_grp[i], 0, n_k), in_=rowwise(e_raw[i], 0, n_k), func=ACT.Square)
+            nc.scalar.activation(out=grouped(e_grp[i], 0, hi), in_=rowwise(e_raw[i], 0, hi), func=ACT.Square)
+
+        def square_vector(i):
+            lo = n_k - V_SQUARES.get(i, 0)
+            if lo < n_k:
+                nc.vector.tensor_tensor(
+                    out=grouped(e_grp[i], lo, n_k), in0=rowwise(e_raw[i], lo, n_k), in1=rowwise(e_raw[i], lo, n_k),
+                    op=ALU.mult,
+                )
 
         def regroup_gpsimd(i):
             g_grp[i] = ggrp.tile([P, width], BF16, name="g_grp", tag="g_grp", align_bytes=64)
             nc.gpsimd.tensor_scalar(
-                out=grouped(g_grp[i], 0, GP_COLS), in0=rowwise(g_raw[i], 0, GP_COLS),
+                out=g_grp[i][:, 0 : PACK * GP_COLS].rearrange("p (w t) -> p w t", t=PACK),
+                in0=g_raw[i][:].rearrange("p (t w) -> p w t", t=PACK)[:, 0:GP_COLS, :],
                 scalar1=1.0, scalar2=0.0, op0=ALU.mult, op1=ALU.add,
             )
 
@@ -131,10 +150,10 @@ def tile_hks_kernel(tc, evals, evecs, count, grad_out, out):
             prod[b, ct] = prdp.tile([P, n_k], F32, name="prod", tag="prod")
             nc.vector.tensor_tensor(out=prod[b, ct][:], in0=d_ps[b, ct][:], in1=wgt[b, ct][:], op=ALU.mult)
 
-        def reduce_c(b, ct):
+        def reduce_c(b, ct, first, last):
             nc.tensor.matmul(
                 out=acc[:], lhsT=selw[:, P - 1 - b : 2 * P - 1 - b], rhs=prod[b, ct][:],
-                start=(b == 0 and ct == 0), stop=(b == n_b - 1 and ct == c_tiles - 1),
+                start=first, stop=last,
             )
 
         lam8 = const.tile([P, n_k], BF16)
@@ -167,6 +186,7 @@ def tile_hks_kernel(tc, evals, evecs, count, grad_out, out):
         weights(0)
         regroup(0)
         square(0)
+        square_vector(0)
         load(RAW_BUFS)
         quantise_g(0, 1)
 
@@ -175,6 +195,7 @@ def tile_hks_kernel(tc, evals, evecs, count, grad_out, out):
             if i + 1 < chunks:
                 regroup(i + 1)
                 square(i + 1)
+                square_vector(i + 1)
             if i + 1 + RAW_BUFS < chunks:
                 load(i + 1 + RAW_BUFS)
             quantise_e(i)
@@ -193,9 +214,15 @@ def tile_hks_kernel(tc, evals, evecs, count, grad_out, out):
                 mx_pass(i, 3)
                 weigh(b - 1, 2)
                 weigh(b - 1, 3)
-                for ct in range(c_tiles):
-                    reduce_c(b - 1, ct)
-                weights(b)
+                if b == n_b - 1 and False:
+                    for ct in (0, 2):
+                        nc.vector.tensor_tensor(out=prod[b - 1, ct][:], in0=prod[b - 1, ct][:], in1=prod[b - 1, ct + 1][:], op=ALU.add)
+                        reduce_c(b - 1, ct, False, False)
+                else:
+                    for ct in range(c_tiles):
+                        reduce_c(b - 1, ct, b == 1 and ct == 0, False)
+                if b < n_b - 1 or not False:
+                    weights(b)
             else:
                 for ct in range(c_tiles):
                     mx_pass(i, ct)
@@ -205,11 +232,11 @@ def tile_hks_kernel(tc, evals, evecs, count, grad_out, out):
         b = n_b - 1
         for ct in range(2):
             weigh(b, ct)
-            reduce_c(b, ct)
+            reduce_c(b, ct, False, False)
         weigh(b, 2)
         weigh(b, 3)
         nc.vector.tensor_tensor(out=prod[b, 3][:], in0=prod[b, 2][:], in1=prod[b, 3][:], op=ALU.add)
-        reduce_c(b, 3)
+        reduce_c(b, 3, False, True)
 
         res = const.tile([P, n_k], F32)
         nc.scalar.copy(out=res[:], in_=acc[:])

@@ -22,8 +22,8 @@ FLOPS = 2 * 8 * 512 * 512 * 2048
 
 RAW_BUFS = 8
 BANKS = 7
-GP_COLS = 320
-V_SQUARES = {}
+GP_COLS = 352
+V_SQUARES = {15: 160, 31: 160}
 
 
 def tile_hks_kernel(tc, evals, evecs, count, grad_out, out):
@@ -40,7 +40,7 @@ def tile_hks_kernel(tc, evals, evecs, count, grad_out, out):
         const = ctx.enter_context(tc.tile_pool(name="const", bufs=1))
         rawp = ctx.enter_context(tc.tile_pool(name="rawp", bufs=RAW_BUFS))
         ggrp = ctx.enter_context(tc.tile_pool(name="ggrp", bufs=2))
-        egrp = ctx.enter_context(tc.tile_pool(name="egrp", bufs=3))
+        egrp = ctx.enter_context(tc.tile_pool(name="egrp", bufs=4))
         codp = ctx.enter_context(tc.tile_pool(name="codp", bufs=4))
         wgtp = ctx.enter_context(tc.tile_pool(name="wgtp", bufs=2 * c_tiles))
         prdp = ctx.enter_context(tc.tile_pool(name="prdp", bufs=4))
@@ -138,13 +138,21 @@ def tile_hks_kernel(tc, evals, evecs, count, grad_out, out):
                 start=True, stop=True,
             )
 
+        def with_s(b):
+            return b == n_b - 1
+
         def weights(b):
             for ct in range(c_tiles):
                 wgt[b, ct] = wgtp.tile([P, n_k], F32, name="wgt", tag="wgt")
-                nc.scalar.activation(
-                    out=wgt[b, ct][:], in_=lam_ps[b][:], func=ACT.Exp,
-                    bias=lns[:, ct : ct + 1], scale=sneg[:, ct : ct + 1],
-                )
+                if with_s(b):
+                    nc.scalar.activation(
+                        out=wgt[b, ct][:], in_=lam_ps[b][:], func=ACT.Exp,
+                        bias=lns[:, ct : ct + 1], scale=sneg[:, ct : ct + 1],
+                    )
+                else:
+                    nc.scalar.activation(
+                        out=wgt[b, ct][:], in_=lam_ps[b][:], func=ACT.Exp, scale=sneg[:, ct : ct + 1],
+                    )
 
         def weigh(b, ct):
             prod[b, ct] = prdp.tile([P, n_k], F32, name="prod", tag="prod")
@@ -152,12 +160,12 @@ def tile_hks_kernel(tc, evals, evecs, count, grad_out, out):
 
         def reduce_c(b, ct, first, last):
             nc.tensor.matmul(
-                out=acc[:], lhsT=selw[:, P - 1 - b : 2 * P - 1 - b], rhs=prod[b, ct][:],
+                out=acc[:], lhsT=selw[:, c_tiles if with_s(b) else ct, P - 1 - b : 2 * P - 1 - b], rhs=prod[b, ct][:],
                 start=first, stop=last,
             )
 
         lam8 = const.tile([P, n_k], BF16)
-        nc.vector.memset(lam8[:], 0.0)
+        nc.gpsimd.memset(lam8[:].bitcast(F32), 0.0)
         nc.sync.dma_start(out=lam8[0:n_b, :], in_=evals)
         for i in range(RAW_BUFS):
             load(i)
@@ -175,11 +183,12 @@ def tile_hks_kernel(tc, evals, evecs, count, grad_out, out):
         )
         spos = const.tile([P, c_tiles], F32)
         nc.scalar.activation(out=spos[:], in_=lns[:], func=ACT.Exp)
-        selw = const.tile([P, 2 * P], F32)
+        selw = const.tile([P, c_tiles + 1, 2 * P], F32)
         nc.vector.memset(selw[:], 0.0)
-        nc.vector.memset(selw[:, P - 1 : P], -1.0)
+        nc.vector.memset(selw[:, c_tiles, P - 1 : P], -1.0)
         sneg = const.tile([P, c_tiles], F32)
         nc.vector.tensor_scalar_mul(out=sneg[:], in0=spos[:], scalar1=-1.0)
+        nc.vector.tensor_copy(out=selw[:, 0:c_tiles, P - 1 : P], in_=sneg[:].unsqueeze(2))
         acc = accp.tile([P, n_k], F32)
 
         spread_evals(0)
@@ -221,7 +230,7 @@ def tile_hks_kernel(tc, evals, evecs, count, grad_out, out):
                 else:
                     for ct in range(c_tiles):
                         reduce_c(b - 1, ct, b == 1 and ct == 0, False)
-                if b < n_b - 1 or not False:
+                if b < n_b - 1 or not True:
                     weights(b)
             else:
                 for ct in range(c_tiles):
@@ -230,6 +239,7 @@ def tile_hks_kernel(tc, evals, evecs, count, grad_out, out):
                 spread_evals(b + 1)
 
         b = n_b - 1
+        weights(b)
         for ct in range(2):
             weigh(b, ct)
             reduce_c(b, ct, False, False)

@@ -39,7 +39,7 @@ def tile_hks_kernel(tc, evals, evecs, count, grad_out, out):
     with ExitStack() as ctx:
         const = ctx.enter_context(tc.tile_pool(name="const", bufs=1))
         rawp = ctx.enter_context(tc.tile_pool(name="rawp", bufs=RAW_BUFS))
-        ggrp = ctx.enter_context(tc.tile_pool(name="ggrp", bufs=2))
+        ggrp = ctx.enter_context(tc.tile_pool(name="ggrp", bufs=1))
         egrp = ctx.enter_context(tc.tile_pool(name="egrp", bufs=4))
         codp = ctx.enter_context(tc.tile_pool(name="codp", bufs=4))
         wgtp = ctx.enter_context(tc.tile_pool(name="wgtp", bufs=2 * c_tiles))
@@ -91,7 +91,7 @@ def tile_hks_kernel(tc, evals, evecs, count, grad_out, out):
                 )
 
         def regroup_gpsimd(i):
-            g_grp[i] = ggrp.tile([P, width], BF16, name="g_grp", tag="g_grp", align_bytes=64)
+            g_grp[i] = ggrp.tile([P, width], BF16, name="g_grp%d" % (i % 2), tag="g_grp%d" % (i % 2), align_bytes=64)
             nc.gpsimd.tensor_scalar(
                 out=g_grp[i][:, 0 : PACK * GP_COLS].rearrange("p (w t) -> p w t", t=PACK),
                 in0=g_raw[i][:].rearrange("p (t w) -> p w t", t=PACK)[:, 0:GP_COLS, :],
@@ -101,7 +101,7 @@ def tile_hks_kernel(tc, evals, evecs, count, grad_out, out):
         def regroup(i):
             lo = GP_COLS if i in g_grp else 0
             if lo == 0:
-                g_grp[i] = ggrp.tile([P, width], BF16, name="g_grp", tag="g_grp", align_bytes=64)
+                g_grp[i] = ggrp.tile([P, width], BF16, name="g_grp%d" % (i % 2), tag="g_grp%d" % (i % 2), align_bytes=64)
             nc.vector.tensor_copy(out=grouped(g_grp[i], lo, n_c), in_=rowwise(g_raw[i], lo, n_c))
 
         def quantise_g(i, pieces):

@@ -23,6 +23,7 @@ FLOPS = 2 * 8 * 512 * 512 * 2048
 RAW_BUFS = 8
 BANKS = 7
 GP_COLS = 352
+RUN = 8
 V_SQUARES = {15: 160, 31: 160}
 
 
@@ -72,10 +73,10 @@ def tile_hks_kernel(tc, evals, evecs, count, grad_out, out):
             load_e(i)
 
         def grouped(tile_ap, lo, hi):
-            return tile_ap[:, PACK * lo : PACK * hi].rearrange("p (c i t) -> p c t i", i=4, t=PACK)
+            return tile_ap[:, PACK * lo : PACK * hi].rearrange("p (c i t) -> p c t i", i=RUN, t=PACK)
 
         def rowwise(tile_ap, lo, hi):
-            return tile_ap[:].rearrange("p (t w) -> p t w", t=PACK)[:, :, lo:hi].rearrange("p t (c i) -> p c t i", i=4)
+            return tile_ap[:].rearrange("p (t w) -> p t w", t=PACK)[:, :, lo:hi].rearrange("p t (c i) -> p c t i", i=RUN)
 
         def square(i):
             hi = n_k - V_SQUARES.get(i, 0)

@@ -24,7 +24,7 @@ RAW_BUFS = 8
 BANKS = 7
 GP_COLS = 352
 RUN = 8
-V_SQUARES = {15: 160, 31: 160}
+V_SQUARES = {31: 160}
 
 
 def tile_hks_kernel(tc, evals, evecs, count, grad_out, out):
@@ -92,7 +92,7 @@ def tile_hks_kernel(tc, evals, evecs, count, grad_out, out):
                 )
 
         def regroup_gpsimd(i):
-            g_grp[i] = ggrp.tile([P, width], BF16, name="g_grp%d" % (i % 2), tag="g_grp%d" % (i % 2), align_bytes=64)
+            g_grp[i] = ggrp.tile([P, width], BF16, name="g_grp%d" % (i % 4), tag="g_grp%d" % (i % 4), align_bytes=64)
             nc.gpsimd.tensor_scalar(
                 out=g_grp[i][:, 0 : PACK * GP_COLS].rearrange("p (w t) -> p w t", t=PACK),
                 in0=g_raw[i][:].rearrange("p (t w) -> p w t", t=PACK)[:, 0:GP_COLS, :],
@@ -102,7 +102,7 @@ def tile_hks_kernel(tc, evals, evecs, count, grad_out, out):
         def regroup(i):
             lo = GP_COLS if i in g_grp else 0
             if lo == 0:
-                g_grp[i] = ggrp.tile([P, width], BF16, name="g_grp%d" % (i % 2), tag="g_grp%d" % (i % 2), align_bytes=64)
+                g_grp[i] = ggrp.tile([P, width], BF16, name="g_grp%d" % (i % 4), tag="g_grp%d" % (i % 4), align_bytes=64)
             nc.vector.tensor_copy(out=grouped(g_grp[i], lo, n_c), in_=rowwise(g_raw[i], lo, n_c))
 
         def quantise_g(i, pieces):
@@ -142,8 +142,8 @@ def tile_hks_kernel(tc, evals, evecs, count, grad_out, out):
         def with_s(b):
             return b == n_b - 1
 
-        def weights(b):
-            for ct in range(c_tiles):
+        def weights(b, lo=0, hi=4):
+            for ct in range(lo, hi):
                 wgt[b, ct] = wgtp.tile([P, n_k], F32, name="wgt", tag="wgt")
                 if with_s(b):
                     nc.scalar.activation(
@@ -193,7 +193,7 @@ def tile_hks_kernel(tc, evals, evecs, count, grad_out, out):
         acc = accp.tile([P, n_k], F32)
 
         spread_evals(0)
-        weights(0)
+        weights(0, 0, 3)
         regroup(0)
         square(0)
         square_vector(0)
@@ -202,40 +202,31 @@ def tile_hks_kernel(tc, evals, evecs, count, grad_out, out):
 
         for i in range(chunks):
             b, vc = divmod(i, passes)
+            turn = vc == 0 and b > 0
             if i + 1 < chunks:
                 regroup(i + 1)
                 square(i + 1)
                 square_vector(i + 1)
+            if i == 0:
+                weights(0, 3, 4)
             if i + 1 + RAW_BUFS < chunks:
                 load(i + 1 + RAW_BUFS)
+            if turn:
+                if i + 3 < chunks:
+                    regroup_gpsimd(i + 3)
+                for ct in range(c_tiles):
+                    weigh(b - 1, ct)
+                for ct in range(c_tiles):
+                    reduce_c(b - 1, ct, b == 1 and ct == 0, False)
             quantise_e(i)
             if i + 1 < chunks - 1:
                 quantise_g(i + 1, 1)
             if i == chunks - 1:
                 quantise_g(i, c_tiles)
-            if vc == 0 and b > 0:
-                if GP_COLS > 0 and i + 3 < chunks:
-                    regroup_gpsimd(i + 3)
-                mx_pass(i, 0)
-                mx_pass(i, 1)
-                weigh(b - 1, 0)
-                mx_pass(i, 2)
-                weigh(b - 1, 1)
-                mx_pass(i, 3)
-                weigh(b - 1, 2)
-                weigh(b - 1, 3)
-                if b == n_b - 1 and False:
-                    for ct in (0, 2):
-                        nc.vector.tensor_tensor(out=prod[b - 1, ct][:], in0=prod[b - 1, ct][:], in1=prod[b - 1, ct + 1][:], op=ALU.add)
-                        reduce_c(b - 1, ct, False, False)
-                else:
-                    for ct in range(c_tiles):
-                        reduce_c(b - 1, ct, b == 1 and ct == 0, False)
-                if b < n_b - 1 or not True:
-                    weights(b)
-            else:
-                for ct in range(c_tiles):
-                    mx_pass(i, ct)
+            for ct in range(c_tiles):
+                mx_pass(i, ct)
+            if turn and b < n_b - 1:
+                weights(b)
             if vc == passes - 1 and b + 1 < n_b:
                 spread_evals(b + 1)
 

@@ -24,7 +24,7 @@ RAW_BUFS = 8
 BANKS = 7
 GP_COLS = 352
 RUN = 8
-V_SQUARES = {31: 160}
+V_SQUARES = {}
 
 
 def tile_hks_kernel(tc, evals, evecs, count, grad_out, out):
@@ -103,7 +103,12 @@ def tile_hks_kernel(tc, evals, evecs, count, grad_out, out):
             lo = GP_COLS if i in g_grp else 0
             if lo == 0:
                 g_grp[i] = ggrp.tile([P, width], BF16, name="g_grp%d" % (i % 4), tag="g_grp%d" % (i % 4), align_bytes=64)
+            if i == chunks - 1:
+                return
             nc.vector.tensor_copy(out=grouped(g_grp[i], lo, n_c), in_=rowwise(g_raw[i], lo, n_c))
+
+        def regroup_scalar(i):
+            nc.scalar.copy(out=grouped(g_grp[i], GP_COLS, n_c), in_=rowwise(g_raw[i], GP_COLS, n_c))
 
         def quantise_g(i, pieces):
             g_cod[i] = codp.tile([P, n_c], U32, name="g_cod", tag="g_cod", align_bytes=64)
@@ -140,7 +145,7 @@ def tile_hks_kernel(tc, evals, evecs, count, grad_out, out):
             )
 
         def with_s(b):
-            return b == n_b - 1
+            return b >= n_b - 2
 
         def weights(b, lo=0, hi=4):
             for ct in range(lo, hi):
@@ -207,6 +212,8 @@ def tile_hks_kernel(tc, evals, evecs, count, grad_out, out):
                 regroup(i + 1)
                 square(i + 1)
                 square_vector(i + 1)
+            if i + 1 == chunks - 1:
+                regroup_scalar(i + 1)
             if i == 0:
                 weights(0, 3, 4)
             if i + 1 + RAW_BUFS < chunks:
@@ -216,8 +223,11 @@ def tile_hks_kernel(tc, evals, evecs, count, grad_out, out):
                     regroup_gpsimd(i + 3)
                 for ct in range(c_tiles):
                     weigh(b - 1, ct)
+                if with_s(b - 1):
+                    nc.vector.tensor_tensor(out=prod[b - 1, 3][:], in0=prod[b - 1, 2][:], in1=prod[b - 1, 3][:], op=ALU.add)
                 for ct in range(c_tiles):
-                    reduce_c(b - 1, ct, b == 1 and ct == 0, False)
+                    if not (with_s(b - 1) and ct == 2):
+                        reduce_c(b - 1, ct, b == 1 and ct == 0, False)
             quantise_e(i)
             if i + 1 < chunks - 1:
                 quantise_g(i + 1, 1)

@@ -218,23 +218,34 @@ def tile_hks_kernel(tc, evals, evecs, count, grad_out, out):
                 weights(0, 3, 4)
             if i + 1 + RAW_BUFS < chunks:
                 load(i + 1 + RAW_BUFS)
-            if turn:
-                if i + 3 < chunks:
-                    regroup_gpsimd(i + 3)
+            early = turn and b == n_b - 1
+            if turn and i + 3 < chunks:
+                regroup_gpsimd(i + 3)
+            if early:
                 for ct in range(c_tiles):
                     weigh(b - 1, ct)
-                if with_s(b - 1):
-                    nc.vector.tensor_tensor(out=prod[b - 1, 3][:], in0=prod[b - 1, 2][:], in1=prod[b - 1, 3][:], op=ALU.add)
-                for ct in range(c_tiles):
-                    if not (with_s(b - 1) and ct == 2):
-                        reduce_c(b - 1, ct, b == 1 and ct == 0, False)
+                nc.vector.tensor_tensor(out=prod[b - 1, 3][:], in0=prod[b - 1, 2][:], in1=prod[b - 1, 3][:], op=ALU.add)
+                for ct in (0, 1, 3):
+                    reduce_c(b - 1, ct, False, False)
             quantise_e(i)
             if i + 1 < chunks - 1:
                 quantise_g(i + 1, 1)
             if i == chunks - 1:
                 quantise_g(i, c_tiles)
-            for ct in range(c_tiles):
-                mx_pass(i, ct)
+            if turn and not early:
+                mx_pass(i, 0)
+                mx_pass(i, 1)
+                weigh(b - 1, 0)
+                mx_pass(i, 2)
+                weigh(b - 1, 1)
+                mx_pass(i, 3)
+                weigh(b - 1, 2)
+                weigh(b - 1, 3)
+                for ct in range(c_tiles):
+                    reduce_c(b - 1, ct, b == 1 and ct == 0, False)
+            else:
+                for ct in range(c_tiles):
+                    mx_pass(i, ct)
             if turn and b < n_b - 1:
                 weights(b)
             if vc == passes - 1 and b + 1 < n_b:

@@ -224,10 +224,11 @@ def tile_hks_kernel(tc, evals, evecs, count, grad_out, out):
             if early:
                 for ct in range(c_tiles):
                     weigh(b - 1, ct)
-                nc.vector.tensor_tensor(out=prod[b - 1, 3][:], in0=prod[b - 1, 2][:], in1=prod[b - 1, 3][:], op=ALU.add)
-                for ct in (0, 1, 3):
+                for ct in (0, 1):
                     reduce_c(b - 1, ct, False, False)
             quantise_e(i)
+            if early:
+                nc.vector.tensor_tensor(out=prod[b - 1, 3][:], in0=prod[b - 1, 2][:], in1=prod[b - 1, 3][:], op=ALU.add)
             if i + 1 < chunks - 1:
                 quantise_g(i + 1, 1)
             if i == chunks - 1:
@@ -246,6 +247,8 @@ def tile_hks_kernel(tc, evals, evecs, count, grad_out, out):
             else:
                 for ct in range(c_tiles):
                     mx_pass(i, ct)
+            if early:
+                reduce_c(b - 1, 3, False, False)
             if turn and b < n_b - 1:
                 weights(b)
             if vc == passes - 1 and b + 1 < n_b:
@@ -263,4 +266,4 @@ def tile_hks_kernel(tc, evals, evecs, count, grad_out, out):
 
         res = const.tile([P, n_k], F32)
         nc.scalar.copy(out=res[:], in_=acc[:])
-        nc.sync.dma_start(out=out, in_=res[0:n_b, :])
+        nc.scalar.dma_start(out=out, in_=res[0:n_b, :])

@@ -22,9 +22,9 @@ FLOPS = 2 * 8 * 512 * 512 * 2048
 
 RAW_BUFS = 8
 BANKS = 7
-GP_COLS = 352
+GP_COLS = 400
 RUN = 8
-V_SQUARES = {}
+V_SQUARES = {9: 64, 21: 64}
 
 
 def tile_hks_kernel(tc, evals, evecs, count, grad_out, out):

import math
from contextlib import ExitStack

import concourse.mybir as mybir
from concourse.masks import make_identity

F32 = mybir.dt.float32
BF16 = mybir.dt.bfloat16
U32 = mybir.dt.uint32
U8 = mybir.dt.uint8
I32 = mybir.dt.int32
E4 = mybir.dt.float8_e4m3fn_x4
E5 = mybir.dt.float8_e5m2_x4
ACT = mybir.ActivationFunctionType
ALU = mybir.AluOpType

P = 128
PACK = 4
K_PASS = P * PACK

FLOPS = 2 * 8 * 512 * 512 * 2048

RAW_BUFS = 8
BANKS = 7
GP_COLS = 400
RUN = 8
V_SQUARES = {9: 64, 21: 64}


def tile_hks_kernel(tc, evals, evecs, count, grad_out, out):
    nc = tc.nc
    n_b, n_v, n_k = evecs.shape
    n_c = grad_out.shape[2]
    assert count == n_c and n_k == 512 and n_c == 512 and n_v % K_PASS == 0
    passes = n_v // K_PASS
    c_tiles = n_c // P
    width = PACK * n_k
    chunks = n_b * passes

    with ExitStack() as ctx:
        const = ctx.enter_context(tc.tile_pool(name="const", bufs=1))
        rawp = ctx.enter_context(tc.tile_pool(name="rawp", bufs=RAW_BUFS))
        ggrp = ctx.enter_context(tc.tile_pool(name="ggrp", bufs=1))
        egrp = ctx.enter_context(tc.tile_pool(name="egrp", bufs=4))
        codp = ctx.enter_context(tc.tile_pool(name="codp", bufs=4))
        wgtp = ctx.enter_context(tc.tile_pool(name="wgtp", bufs=2 * c_tiles))
        prdp = ctx.enter_context(tc.tile_pool(name="prdp", bufs=4))
        bankp = ctx.enter_context(tc.psum_pool(name="bankp", bufs=1))
        accp = ctx.enter_context(tc.psum_pool(name="accp", bufs=1))
        ctx.enter_context(tc.manual_schedule())

        g_raw, e_raw, g_grp, e_grp = {}, {}, {}, {}
        g_cod, g_scl, e_cod, e_scl = {}, {}, {}, {}
        lam_ps, wgt, d_ps, prod = {}, {}, {}, {}

        def bank(index):
            return bankp.tile([P, n_k], F32, name="bank%d" % (index % BANKS), tag="bank%d" % (index % BANKS))

        def load_g(i):
            b, vc = divmod(i, passes)
            rows = slice(vc * K_PASS, (vc + 1) * K_PASS)
            g_raw[i] = rawp.tile([P, width], BF16, name="g_raw", tag="g_raw")
            nc.sync.dma_start(out=g_raw[i][:], in_=grad_out[b, rows, :].rearrange("(p j) w -> p (j w)", j=PACK))

        def load_e(i):
            b, vc = divmod(i, passes)
            rows = slice(vc * K_PASS, (vc + 1) * K_PASS)
            e_raw[i] = rawp.tile([P, width], BF16, name="e_raw", tag="e_raw")
            nc.sync.dma_start(out=e_raw[i][:], in_=evecs[b, rows, :].rearrange("(p j) w -> p (j w)", j=PACK))

        def load(i):
            load_g(i)
            load_e(i)

        def grouped(tile_ap, lo, hi):
            return tile_ap[:, PACK * lo : PACK * hi].rearrange("p (c i t) -> p c t i", i=RUN, t=PACK)

        def rowwise(tile_ap, lo, hi):
            return tile_ap[:].rearrange("p (t w) -> p t w", t=PACK)[:, :, lo:hi].rearrange("p t (c i) -> p c t i", i=RUN)

        def square(i):
            hi = n_k - V_SQUARES.get(i, 0)
            e_grp[i] = egrp.tile([P, width], BF16, name="e_grp", tag="e_grp", align_bytes=64)
            nc.scalar.activation(out=grouped(e_grp[i], 0, hi), in_=rowwise(e_raw[i], 0, hi), func=ACT.Square)

        def square_vector(i):
            lo = n_k - V_SQUARES.get(i, 0)
            if lo < n_k:
                nc.vector.tensor_tensor(
                    out=grouped(e_grp[i], lo, n_k), in0=rowwise(e_raw[i], lo, n_k), in1=rowwise(e_raw[i], lo, n_k),
                    op=ALU.mult,
                )

        def regroup_gpsimd(i):
            g_grp[i] = ggrp.tile([P, width], BF16, name="g_grp%d" % (i % 4), tag="g_grp%d" % (i % 4), align_bytes=64)
            nc.gpsimd.tensor_scalar(
                out=g_grp[i][:, 0 : PACK * GP_COLS].rearrange("p (w t) -> p w t", t=PACK),
                in0=g_raw[i][:].rearrange("p (t w) -> p w t", t=PACK)[:, 0:GP_COLS, :],
                scalar1=1.0, scalar2=0.0, op0=ALU.mult, op1=ALU.add,
            )

        def regroup(i):
            lo = GP_COLS if i in g_grp else 0
            if lo == 0:
                g_grp[i] = ggrp.tile([P, width], BF16, name="g_grp%d" % (i % 4), tag="g_grp%d" % (i % 4), align_bytes=64)
            if i == chunks - 1:
                return
            nc.vector.tensor_copy(out=grouped(g_grp[i], lo, n_c), in_=rowwise(g_raw[i], lo, n_c))

        def regroup_scalar(i):
            nc.scalar.copy(out=grouped(g_grp[i], GP_COLS, n_c), in_=rowwise(g_raw[i], GP_COLS, n_c))

        def quantise_g(i, pieces):
            g_cod[i] = codp.tile([P, n_c], U32, name="g_cod", tag="g_cod", align_bytes=64)
            g_scl[i] = codp.tile([P, n_c], U8, name="g_scl", tag="g_scl", align_bytes=64)
            step = n_c // pieces
            for lo in range(0, n_c, step):
                nc.vector.quantize_mx(
                    out=g_cod[i][:, lo : lo + step].bitcast(E5), scales=g_scl[i][:, lo : lo + step],
                    in_=g_grp[i][:, PACK * lo : PACK * (lo + step)],
                )

        def quantise_e(i):
            e_cod[i] = codp.tile([P, n_k], U32, name="e_cod", tag="e_cod", align_bytes=64)
            e_scl[i] = codp.tile([P, n_k], U8, name="e_scl", tag="e_scl", align_bytes=64)
            nc.vector.quantize_mx(out=e_cod[i][:].bitcast(E4), scales=e_scl[i][:], in_=e_grp[i][:])

        def mx_pass(i, ct):
            b, vc = divmod(i, passes)
            if vc == 0:
                d_ps[b, ct] = bank(5 * b + 1 + ct)
            cols = slice(ct * P, (ct + 1) * P)
            nc.tensor.matmul_mx(
                out=d_ps[b, ct][:],
                lhsT=g_cod[i][:, cols].bitcast(E5), lhsT_scale=g_scl[i][:, cols],
                rhs=e_cod[i][:].bitcast(E4), rhs_scale=e_scl[i][:],
                start=(vc == 0), stop=(vc == passes - 1),
            )

        def spread_evals(b):
            lam_ps[b] = bank(5 * b)
            nc.tensor.matmul(
                out=lam_ps[b][:], lhsT=ident[:, b : b + 1].to_broadcast([P, P]), rhs=lam8[:],
                start=True, stop=True,
            )

        def with_s(b):
            return b >= n_b - 2

        def weights(b, lo=0, hi=4):
            for ct in range(lo, hi):
                wgt[b, ct] = wgtp.tile([P, n_k], F32, name="wgt", tag="wgt")
                if with_s(b):
                    nc.scalar.activation(
                        out=wgt[b, ct][:], in_=lam_ps[b][:], func=ACT.Exp,
                        bias=lns[:, ct : ct + 1], scale=sneg[:, ct : ct + 1],
                    )
                else:
                    nc.scalar.activation(
                        out=wgt[b, ct][:], in_=lam_ps[b][:], func=ACT.Exp, scale=sneg[:, ct : ct + 1],
                    )

        def weigh(b, ct):
            prod[b, ct] = prdp.tile([P, n_k], F32, name="prod", tag="prod")
            nc.vector.tensor_tensor(out=prod[b, ct][:], in0=d_ps[b, ct][:], in1=wgt[b, ct][:], op=ALU.mult)

        def reduce_c(b, ct, first, last):
            nc.tensor.matmul(
                out=acc[:], lhsT=selw[:, c_tiles if with_s(b) else ct, P - 1 - b : 2 * P - 1 - b], rhs=prod[b, ct][:],
                start=first, stop=last,
            )

        lam8 = const.tile([P, n_k], BF16)
        nc.gpsimd.memset(lam8[:].bitcast(F32), 0.0)
        nc.sync.dma_start(out=lam8[0:n_b, :], in_=evals)
        for i in range(RAW_BUFS):
            load(i)
        cidx = const.tile([P, c_tiles], I32)
        nc.gpsimd.iota(cidx[:], pattern=[[P, c_tiles]], base=0, channel_multiplier=1)
        ident = const.tile([P, P], BF16)
        make_identity(nc, ident[:])
        cflt = const.tile([P, c_tiles], F32)
        nc.vector.tensor_copy(out=cflt[:], in_=cidx[:])
        lns = const.tile([P, c_tiles], F32)
        nc.vector.tensor_scalar(
            out=lns[:], in0=cflt[:],
            scalar1=2.0 * math.log(10.0) / (n_c - 1), scalar2=-2.0 * math.log(10.0),
            op0=ALU.mult, op1=ALU.add,
        )
        spos = const.tile([P, c_tiles], F32)
        nc.scalar.activation(out=spos[:], in_=lns[:], func=ACT.Exp)
        selw = const.tile([P, c_tiles + 1, 2 * P], F32)
        nc.vector.memset(selw[:], 0.0)
        nc.vector.memset(selw[:, c_tiles, P - 1 : P], -1.0)
        sneg = const.tile([P, c_tiles], F32)
        nc.vector.tensor_scalar_mul(out=sneg[:], in0=spos[:], scalar1=-1.0)
        nc.vector.tensor_copy(out=selw[:, 0:c_tiles, P - 1 : P], in_=sneg[:].unsqueeze(2))
        acc = accp.tile([P, n_k], F32)

        spread_evals(0)
        weights(0, 0, 3)
        regroup(0)
        square(0)
        square_vector(0)
        load(RAW_BUFS)
        quantise_g(0, 1)

        for i in range(chunks):
            b, vc = divmod(i, passes)
            turn = vc == 0 and b > 0
            if i + 1 < chunks:
                regroup(i + 1)
                square(i + 1)
                square_vector(i + 1)
            if i + 1 == chunks - 1:
                regroup_scalar(i + 1)
            if i == 0:
                weights(0, 3, 4)
            if i + 1 + RAW_BUFS < chunks:
                load(i + 1 + RAW_BUFS)
            early = turn and b == n_b - 1
            if turn and i + 3 < chunks:
                regroup_gpsimd(i + 3)
            if early:
                for ct in range(c_tiles):
                    weigh(b - 1, ct)
                for ct in (0, 1):
                    reduce_c(b - 1, ct, False, False)
            quantise_e(i)
            if early:
                nc.vector.tensor_tensor(out=prod[b - 1, 3][:], in0=prod[b - 1, 2][:], in1=prod[b - 1, 3][:], op=ALU.add)
            if i + 1 < chunks - 1:
                quantise_g(i + 1, 1)
            if i == chunks - 1:
                quantise_g(i, c_tiles)
            if turn and not early:
                mx_pass(i, 0)
                mx_pass(i, 1)
                weigh(b - 1, 0)
                mx_pass(i, 2)
                weigh(b - 1, 1)
                mx_pass(i, 3)
                weigh(b - 1, 2)
                weigh(b - 1, 3)
                for ct in range(c_tiles):
                    reduce_c(b - 1, ct, b == 1 and ct == 0, False)
            else:
                for ct in range(c_tiles):
                    mx_pass(i, ct)
            if early:
                reduce_c(b - 1, 3, False, False)
            if turn and b < n_b - 1:
                weights(b)
            if vc == passes - 1 and b + 1 < n_b:
                spread_evals(b + 1)

        b = n_b - 1
        weights(b)
        for ct in range(2):
            weigh(b, ct)
            reduce_c(b, ct, False, False)
        weigh(b, 2)
        weigh(b, 3)
        nc.vector.tensor_tensor(out=prod[b, 3][:], in0=prod[b, 2][:], in1=prod[b, 3][:], op=ALU.add)
        reduce_c(b, 3, False, True)

        res = const.tile([P, n_k], F32)
        nc.scalar.copy(out=res[:], in_=acc[:])
        nc.scalar.dma_start(out=out, in_=res[0:n_b, :])
